import numpy as np
import ml_dtypes

BF16 = ml_dtypes.bfloat16


def bf(x):
    return np.asarray(x, np.float32).astype(BF16)


def f32(x):
    return np.asarray(x, np.float32)


def f64(x):
    return np.asarray(x).astype(np.float64)


def striped(idx):
    return np.tile(idx.reshape(-1, 16).T, (8, 1))


C, HALF, S, N = 128, 64, 4096, 512
ROPE_BASE = 10000.0


def rope_tables():
    freqs = np.exp(np.arange(HALF, dtype=np.float64) * -(np.log(ROPE_BASE) / HALF))
    t = freqs[:, None] * np.arange(N, dtype=np.float64)[None, :]
    cos_t = np.concatenate([np.cos(t), np.cos(t)], axis=0)
    sin_s = np.concatenate([-np.sin(t), np.sin(t)], axis=0)
    return cos_t, sin_s


def setup_inputs():
    cos_t, sin_s = rope_tables()
    return {"base": f32(np.random.standard_normal((C, S))), "k": f32(np.random.standard_normal((C, N))), "cos_t": f32(cos_t), "sin_s": f32(sin_s), "offs": striped(np.random.permutation(S)[:N])}


def reference(base, k, cos_t, sin_s, offs):
    idx = offs[:16].T.reshape(-1)
    kk = f64(k)
    partner = np.concatenate([kk[HALF:], kk[:HALF]], axis=0)
    out = f64(base).copy()
    out[:, idx] = kk * f64(cos_t) + partner * f64(sin_s)
    return out

@@ -1,0 +1,38 @@
+import concourse.mybir as mybir
+
+F32 = mybir.dt.float32
+U16 = mybir.dt.uint16
+MULT = mybir.AluOpType.mult
+ADD = mybir.AluOpType.add
+
+FEATURES = 128
+HALF = FEATURES // 2
+SLOTS = 4096
+KEYS = 512
+
+
+def tile_chunkedselfattention_kernel(tc, base, k, cos_t, sin_s, offs, out):
+    nc = tc.nc
+    with tc.tile_pool(name="held", bufs=1) as held:
+        offsets = held.tile([FEATURES, KEYS // 16], U16, name="offsets")
+        keys = held.tile([FEATURES, KEYS], F32, name="keys")
+        partner = held.tile([FEATURES, KEYS], F32, name="partner")
+        cosines = held.tile([FEATURES, KEYS], F32, name="cosines")
+        sines = held.tile([FEATURES, KEYS], F32, name="sines")
+        cache = held.tile([FEATURES, SLOTS], F32, name="cache")
+        straight = held.tile([FEATURES, KEYS], F32, name="straight")
+        crossed = held.tile([FEATURES, KEYS], F32, name="crossed")
+
+        nc.sync.dma_start(offsets[:], offs)
+        nc.sync.dma_start(keys[:], k)
+        nc.sync.dma_start(cosines[:], cos_t)
+        nc.sync.dma_start(partner[0:HALF, :], k[HALF:FEATURES, :])
+        nc.sync.dma_start(partner[HALF:FEATURES, :], k[0:HALF, :])
+        nc.sync.dma_start(sines[:], sin_s)
+        nc.sync.dma_start(cache[:], base)
+
+        nc.vector.tensor_tensor(straight[:], keys[:], cosines[:], MULT)
+        nc.vector.tensor_tensor(crossed[:], partner[:], sines[:], MULT)
+        nc.vector.tensor_tensor(cache[:].indirect(offsets[:]), straight[:], crossed[:], ADD)
+
+        nc.sync.dma_start(out, cache[:])

@@ -8,6 +8,7 @@ ADD = mybir.AluOpType.add
 FEATURES = 128
 HALF = FEATURES // 2
 SLOTS = 4096
+MIDDLE = SLOTS // 2
 KEYS = 512
 
 
@@ -26,13 +27,15 @@ def tile_chunkedselfattention_kernel(tc, base, k, cos_t, sin_s, offs, out):
         nc.sync.dma_start(offsets[:], offs)
         nc.sync.dma_start(keys[:], k)
         nc.sync.dma_start(cosines[:], cos_t)
-        nc.sync.dma_start(partner[0:HALF, :], k[HALF:FEATURES, :])
-        nc.sync.dma_start(partner[HALF:FEATURES, :], k[0:HALF, :])
-        nc.sync.dma_start(sines[:], sin_s)
-        nc.sync.dma_start(cache[:], base)
+        nc.scalar.dma_start(partner[0:HALF, :], k[HALF:FEATURES, :])
+        nc.scalar.dma_start(partner[HALF:FEATURES, :], k[0:HALF, :])
+        nc.scalar.dma_start(sines[:], sin_s)
+        nc.sync.dma_start(cache[:, 0:MIDDLE], base[:, 0:MIDDLE])
+        nc.scalar.dma_start(cache[:, MIDDLE:SLOTS], base[:, MIDDLE:SLOTS])
 
         nc.vector.tensor_tensor(straight[:], keys[:], cosines[:], MULT)
         nc.vector.tensor_tensor(crossed[:], partner[:], sines[:], MULT)
         nc.vector.tensor_tensor(cache[:].indirect(offsets[:]), straight[:], crossed[:], ADD)
 
-        nc.sync.dma_start(out, cache[:])
+        nc.sync.dma_start(out[:, 0:MIDDLE], cache[:, 0:MIDDLE])
+        nc.scalar.dma_start(out[:, MIDDLE:SLOTS], cache[:, MIDDLE:SLOTS])

@@ -4,38 +4,53 @@ F32 = mybir.dt.float32
 U16 = mybir.dt.uint16
 MULT = mybir.AluOpType.mult
 ADD = mybir.AluOpType.add
+NOT_EQUAL = mybir.AluOpType.not_equal
 
 FEATURES = 128
 HALF = FEATURES // 2
 SLOTS = 4096
-MIDDLE = SLOTS // 2
 KEYS = 512
+
+FLOPS = 3 * FEATURES * KEYS
 
 
 def tile_chunkedselfattention_kernel(tc, base, k, cos_t, sin_s, offs, out):
     nc = tc.nc
-    with tc.tile_pool(name="held", bufs=1) as held:
+    with (
+        tc.tile_pool(name="held", bufs=1) as held,
+        tc.psum_pool(name="psum", bufs=1) as psum,
+    ):
         offsets = held.tile([FEATURES, KEYS // 16], U16, name="offsets")
         keys = held.tile([FEATURES, KEYS], F32, name="keys")
-        partner = held.tile([FEATURES, KEYS], F32, name="partner")
         cosines = held.tile([FEATURES, KEYS], F32, name="cosines")
         sines = held.tile([FEATURES, KEYS], F32, name="sines")
         cache = held.tile([FEATURES, SLOTS], F32, name="cache")
+        swap = held.tile([FEATURES, FEATURES], F32, name="swap")
         straight = held.tile([FEATURES, KEYS], F32, name="straight")
         crossed = held.tile([FEATURES, KEYS], F32, name="crossed")
+        partner = psum.tile([FEATURES, KEYS], F32, name="partner")
 
         nc.sync.dma_start(offsets[:], offs)
         nc.sync.dma_start(keys[:], k)
         nc.sync.dma_start(cosines[:], cos_t)
-        nc.scalar.dma_start(partner[0:HALF, :], k[HALF:FEATURES, :])
-        nc.scalar.dma_start(partner[HALF:FEATURES, :], k[0:HALF, :])
-        nc.scalar.dma_start(sines[:], sin_s)
-        nc.sync.dma_start(cache[:, 0:MIDDLE], base[:, 0:MIDDLE])
-        nc.scalar.dma_start(cache[:, MIDDLE:SLOTS], base[:, MIDDLE:SLOTS])
+        nc.sync.dma_start(sines[:], sin_s)
+        nc.sync.dma_start(cache[:], base)
+
+        nc.gpsimd.memset(swap[:], 0.0)
+        for distance in (HALF, -HALF):
+            nc.gpsimd.affine_select(
+                out=swap[:],
+                in_=swap[:],
+                compare_op=NOT_EQUAL,
+                fill=1.0,
+                base=distance,
+                pattern=[[-1, FEATURES]],
+                channel_multiplier=1,
+            )
+        nc.tensor.matmul(partner[:], swap[:], keys[:], start=True, stop=True)
 
         nc.vector.tensor_tensor(straight[:], keys[:], cosines[:], MULT)
         nc.vector.tensor_tensor(crossed[:], partner[:], sines[:], MULT)
         nc.vector.tensor_tensor(cache[:].indirect(offsets[:]), straight[:], crossed[:], ADD)
 
-        nc.sync.dma_start(out[:, 0:MIDDLE], cache[:, 0:MIDDLE])
-        nc.scalar.dma_start(out[:, MIDDLE:SLOTS], cache[:, MIDDLE:SLOTS])
+        nc.sync.dma_start(out, cache[:])

@@ -10,6 +10,8 @@ FEATURES = 128
 HALF = FEATURES // 2
 SLOTS = 4096
 KEYS = 512
+WINDOWS = 2
+OWNED = SLOTS // WINDOWS
 
 FLOPS = 3 * FEATURES * KEYS
 
@@ -24,7 +26,7 @@ def tile_chunkedselfattention_kernel(tc, base, k, cos_t, sin_s, offs, out):
         keys = held.tile([FEATURES, KEYS], F32, name="keys")
         cosines = held.tile([FEATURES, KEYS], F32, name="cosines")
         sines = held.tile([FEATURES, KEYS], F32, name="sines")
-        cache = held.tile([FEATURES, SLOTS], F32, name="cache")
+        windows = [held.tile([FEATURES, SLOTS], F32, name=f"window{w}") for w in range(WINDOWS)]
         swap = held.tile([FEATURES, FEATURES], F32, name="swap")
         straight = held.tile([FEATURES, KEYS], F32, name="straight")
         crossed = held.tile([FEATURES, KEYS], F32, name="crossed")
@@ -34,7 +36,9 @@ def tile_chunkedselfattention_kernel(tc, base, k, cos_t, sin_s, offs, out):
         nc.sync.dma_start(keys[:], k)
         nc.sync.dma_start(cosines[:], cos_t)
         nc.sync.dma_start(sines[:], sin_s)
-        nc.sync.dma_start(cache[:], base)
+        for w in range(WINDOWS):
+            owned = slice(w * OWNED, (w + 1) * OWNED)
+            nc.sync.dma_start(windows[w][:, owned], base[:, owned])
 
         nc.gpsimd.memset(swap[:], 0.0)
         for distance in (HALF, -HALF):
@@ -51,6 +55,7 @@ def tile_chunkedselfattention_kernel(tc, base, k, cos_t, sin_s, offs, out):
 
         nc.vector.tensor_tensor(straight[:], keys[:], cosines[:], MULT)
         nc.vector.tensor_tensor(crossed[:], partner[:], sines[:], MULT)
-        nc.vector.tensor_tensor(cache[:].indirect(offsets[:]), straight[:], crossed[:], ADD)
-
-        nc.sync.dma_start(out, cache[:])
+        for w in range(WINDOWS):
+            owned = slice(w * OWNED, (w + 1) * OWNED)
+            nc.vector.tensor_tensor(windows[w][:].indirect(offsets[:]), straight[:], crossed[:], ADD)
+            nc.sync.dma_start(out[:, owned], windows[w][:, owned])

@@ -32,10 +32,10 @@ def tile_chunkedselfattention_kernel(tc, base, k, cos_t, sin_s, offs, out):
         crossed = held.tile([FEATURES, KEYS], F32, name="crossed")
         partner = psum.tile([FEATURES, KEYS], F32, name="partner")
 
-        nc.sync.dma_start(offsets[:], offs)
         nc.sync.dma_start(keys[:], k)
         nc.sync.dma_start(cosines[:], cos_t)
         nc.sync.dma_start(sines[:], sin_s)
+        nc.sync.dma_start(offsets[:], offs)
         for w in range(WINDOWS):
             owned = slice(w * OWNED, (w + 1) * OWNED)
             nc.sync.dma_start(windows[w][:, owned], base[:, owned])

@@ -35,10 +35,11 @@ def tile_chunkedselfattention_kernel(tc, base, k, cos_t, sin_s, offs, out):
         nc.sync.dma_start(keys[:], k)
         nc.sync.dma_start(cosines[:], cos_t)
         nc.sync.dma_start(sines[:], sin_s)
-        nc.sync.dma_start(offsets[:], offs)
         for w in range(WINDOWS):
             owned = slice(w * OWNED, (w + 1) * OWNED)
             nc.sync.dma_start(windows[w][:, owned], base[:, owned])
+            if w == 0:
+                nc.sync.dma_start(offsets[:], offs)
 
         nc.gpsimd.memset(swap[:], 0.0)
         for distance in (HALF, -HALF):

@@ -12,6 +12,7 @@ SLOTS = 4096
 KEYS = 512
 WINDOWS = 2
 OWNED = SLOTS // WINDOWS
+BURST = 256
 
 FLOPS = 3 * FEATURES * KEYS
 
@@ -23,10 +24,12 @@ def tile_chunkedselfattention_kernel(tc, base, k, cos_t, sin_s, offs, out):
         tc.psum_pool(name="psum", bufs=1) as psum,
     ):
         offsets = held.tile([FEATURES, KEYS // 16], U16, name="offsets")
-        keys = held.tile([FEATURES, KEYS], F32, name="keys")
-        cosines = held.tile([FEATURES, KEYS], F32, name="cosines")
-        sines = held.tile([FEATURES, KEYS], F32, name="sines")
-        windows = [held.tile([FEATURES, SLOTS], F32, name=f"window{w}") for w in range(WINDOWS)]
+        keys = held.tile([FEATURES, KEYS], F32, name="keys", align_bytes=BURST)
+        cosines = held.tile([FEATURES, KEYS], F32, name="cosines", align_bytes=BURST)
+        sines = held.tile([FEATURES, KEYS], F32, name="sines", align_bytes=BURST)
+        windows = [
+            held.tile([FEATURES, SLOTS], F32, name=f"window{w}", align_bytes=BURST) for w in range(WINDOWS)
+        ]
         swap = held.tile([FEATURES, FEATURES], F32, name="swap")
         straight = held.tile([FEATURES, KEYS], F32, name="straight")
         crossed = held.tile([FEATURES, KEYS], F32, name="crossed")

@@ -10,6 +10,7 @@ FEATURES = 128
 HALF = FEATURES // 2
 SLOTS = 4096
 KEYS = 512
+PIECE = KEYS // 2
 WINDOWS = 2
 OWNED = SLOTS // WINDOWS
 BURST = 256
@@ -33,7 +34,7 @@ def tile_chunkedselfattention_kernel(tc, base, k, cos_t, sin_s, offs, out):
         swap = held.tile([FEATURES, FEATURES], F32, name="swap")
         straight = held.tile([FEATURES, KEYS], F32, name="straight")
         crossed = held.tile([FEATURES, KEYS], F32, name="crossed")
-        partner = psum.tile([FEATURES, KEYS], F32, name="partner")
+        partners = [psum.tile([FEATURES, PIECE], F32, name=f"partner{p}") for p in range(KEYS // PIECE)]
 
         nc.sync.dma_start(keys[:], k)
         nc.sync.dma_start(cosines[:], cos_t)
@@ -55,10 +56,12 @@ def tile_chunkedselfattention_kernel(tc, base, k, cos_t, sin_s, offs, out):
                 pattern=[[-1, FEATURES]],
                 channel_multiplier=1,
             )
-        nc.tensor.matmul(partner[:], swap[:], keys[:], start=True, stop=True)
-
         nc.vector.tensor_tensor(straight[:], keys[:], cosines[:], MULT)
-        nc.vector.tensor_tensor(crossed[:], partner[:], sines[:], MULT)
+        for p, partner in enumerate(partners):
+            piece = slice(p * PIECE, (p + 1) * PIECE)
+            nc.tensor.matmul(partner[:], swap[:], keys[:, piece], start=True, stop=True)
+            nc.vector.tensor_tensor(crossed[:, piece], partner[:], sines[:, piece], MULT)
+
         for w in range(WINDOWS):
             owned = slice(w * OWNED, (w + 1) * OWNED)
             nc.vector.tensor_tensor(windows[w][:].indirect(offsets[:]), straight[:], crossed[:], ADD)

@@ -14,6 +14,7 @@ PIECE = KEYS // 2
 WINDOWS = 2
 OWNED = SLOTS // WINDOWS
 BURST = 256
+WINDOW_BYTES = 4 * SLOTS
 
 FLOPS = 3 * FEATURES * KEYS
 
@@ -29,7 +30,8 @@ def tile_chunkedselfattention_kernel(tc, base, k, cos_t, sin_s, offs, out):
         cosines = held.tile([FEATURES, KEYS], F32, name="cosines", align_bytes=BURST)
         sines = held.tile([FEATURES, KEYS], F32, name="sines", align_bytes=BURST)
         windows = [
-            held.tile([FEATURES, SLOTS], F32, name=f"window{w}", align_bytes=BURST) for w in range(WINDOWS)
+            held.tile([FEATURES, SLOTS], F32, name=f"window{w}", align_bytes=WINDOW_BYTES)
+            for w in range(WINDOWS)
         ]
         swap = held.tile([FEATURES, FEATURES], F32, name="swap")
         straight = held.tile([FEATURES, KEYS], F32, name="straight")

import concourse.mybir as mybir

F32 = mybir.dt.float32
U16 = mybir.dt.uint16
MULT = mybir.AluOpType.mult
ADD = mybir.AluOpType.add
NOT_EQUAL = mybir.AluOpType.not_equal

FEATURES = 128
HALF = FEATURES // 2
SLOTS = 4096
KEYS = 512
PIECE = KEYS // 2
WINDOWS = 2
OWNED = SLOTS // WINDOWS
BURST = 256
WINDOW_BYTES = 4 * SLOTS

FLOPS = 3 * FEATURES * KEYS


def tile_chunkedselfattention_kernel(tc, base, k, cos_t, sin_s, offs, out):
    nc = tc.nc
    with (
        tc.tile_pool(name="held", bufs=1) as held,
        tc.psum_pool(name="psum", bufs=1) as psum,
    ):
        offsets = held.tile([FEATURES, KEYS // 16], U16, name="offsets")
        keys = held.tile([FEATURES, KEYS], F32, name="keys", align_bytes=BURST)
        cosines = held.tile([FEATURES, KEYS], F32, name="cosines", align_bytes=BURST)
        sines = held.tile([FEATURES, KEYS], F32, name="sines", align_bytes=BURST)
        windows = [
            held.tile([FEATURES, SLOTS], F32, name=f"window{w}", align_bytes=WINDOW_BYTES)
            for w in range(WINDOWS)
        ]
        swap = held.tile([FEATURES, FEATURES], F32, name="swap")
        straight = held.tile([FEATURES, KEYS], F32, name="straight")
        crossed = held.tile([FEATURES, KEYS], F32, name="crossed")
        partners = [psum.tile([FEATURES, PIECE], F32, name=f"partner{p}") for p in range(KEYS // PIECE)]

        nc.sync.dma_start(keys[:], k)
        nc.sync.dma_start(cosines[:], cos_t)
        nc.sync.dma_start(sines[:], sin_s)
        for w in range(WINDOWS):
            owned = slice(w * OWNED, (w + 1) * OWNED)
            nc.sync.dma_start(windows[w][:, owned], base[:, owned])
            if w == 0:
                nc.sync.dma_start(offsets[:], offs)

        nc.gpsimd.memset(swap[:], 0.0)
        for distance in (HALF, -HALF):
            nc.gpsimd.affine_select(
                out=swap[:],
                in_=swap[:],
                compare_op=NOT_EQUAL,
                fill=1.0,
                base=distance,
                pattern=[[-1, FEATURES]],
                channel_multiplier=1,
            )
        nc.vector.tensor_tensor(straight[:], keys[:], cosines[:], MULT)
        for p, partner in enumerate(partners):
            piece = slice(p * PIECE, (p + 1) * PIECE)
            nc.tensor.matmul(partner[:], swap[:], keys[:, piece], start=True, stop=True)
            nc.vector.tensor_tensor(crossed[:, piece], partner[:], sines[:, piece], MULT)

        for w in range(WINDOWS):
            owned = slice(w * OWNED, (w + 1) * OWNED)
            nc.vector.tensor_tensor(windows[w][:].indirect(offsets[:]), straight[:], crossed[:], ADD)
            nc.sync.dma_start(out[:, owned], windows[w][:, owned])
